import numpy as np
import ml_dtypes


def mxq(x, axis, fmt="e4m3"):
    dtype, down = {"e4m3": (ml_dtypes.float8_e4m3fn, 7), "e5m2": (ml_dtypes.float8_e5m2, 14)}[fmt]
    v = np.moveaxis(np.asarray(x, np.float32).astype(ml_dtypes.bfloat16).astype(np.float64), axis, -1)
    blocks = v.reshape(v.shape[:-1] + (-1, 32))
    amax = np.abs(blocks).max(-1, keepdims=True)
    byte = np.maximum(np.where(amax > 0, np.frexp(amax)[1] - 1 + 127, 0) - down, 1)
    scale = np.exp2(byte - 127.0)
    codes = (blocks / scale).astype(np.float32).astype(dtype).astype(np.float64)
    return np.moveaxis((codes * scale).reshape(v.shape), -1, axis)


WIDE = False


def mx_kscale(k):
    if not WIDE:
        return np.ones(k)
    levels = np.array([10, -10, 5, -5, 0])
    a = np.random.permutation(np.resize(levels, k // 512 * 4)).reshape(k // 512, 4)
    idx = np.arange(k)
    return np.exp2(a[idx // 512, idx % 128 // 32])


BF16 = ml_dtypes.bfloat16


def bf(x):
    return np.asarray(x, np.float32).astype(BF16)


def f64(x):
    return np.asarray(x).astype(np.float64)


B, C, H, W = 8, 512, 16, 32
N = H * W
SIG = 3.0


def setup_inputs():
    s, t = mx_kscale(C), mx_kscale(C)
    r = np.sqrt(SIG / np.sqrt(C))
    return {
        "q_ir": bf(np.random.standard_normal((B, C, N)) * r / t[:, None]),
        "irSegF": bf(np.random.standard_normal((B, C, H, W)) * s[:, None, None]),
        "Wk_dr": bf(np.random.standard_normal((C, C)) * r / np.sqrt(C) * t[:, None] / s[None, :]),
        "bk_dr": bf(np.random.standard_normal(C) * 0.1 * t),
    }


def reference(q_ir, irSegF, Wk_dr, bk_dr):
    seg = f64(irSegF).reshape(B, C, N)
    key = (mxq(f64(Wk_dr), 1, "e4m3") @ mxq(seg, 1, "e4m3")) + f64(bk_dr)[None, :, None]
    s = mxq(f64(q_ir), 1, "e4m3").transpose(0, 2, 1) @ mxq(key, 1, "e4m3")
    e = np.exp(s - s.max(1, keepdims=True))
    return e / e.sum(1, keepdims=True)

@@ -1,0 +1,171 @@
+from contextlib import ExitStack
+
+import concourse.bass as bass
+import concourse.mybir as mybir
+import concourse.tile as tile
+from concourse.masks import make_identity
+
+F32 = mybir.dt.float32
+BF16 = mybir.dt.bfloat16
+U32 = mybir.dt.uint32
+U8 = mybir.dt.uint8
+FP8X4 = mybir.dt.float8_e4m3fn_x4
+ALU = mybir.AluOpType
+ACT = mybir.ActivationFunctionType
+AX = mybir.AxisListType
+
+P = 128
+B = 8
+C = 512
+N = 512
+PACK = 4
+FLOPS = 2 * 2 * B * C * N * N
+
+SEG_S = [128, 512, 0, 384, 128, 128, 0, 128]
+Q_S = [384, 512, 256, 128, 128, 128, 256, 0]
+NORM_V = [26, 28, 29, 30, 31]
+EVAC_V = [29, 31]
+
+
+def tile_featuremaptransformer_pb_t_kernel(tc, q_ir, irSegF, Wk_dr, bk_dr, out):
+    nc = tc.nc
+    with ExitStack() as ctx:
+        const = ctx.enter_context(tc.tile_pool(name="const", bufs=1))
+        raw = ctx.enter_context(tc.tile_pool(name="raw", bufs=1))
+        grp = ctx.enter_context(tc.tile_pool(name="grp", bufs=3))
+        wrd = ctx.enter_context(tc.tile_pool(name="wrd", bufs=3))
+        stat = ctx.enter_context(tc.tile_pool(name="stat", bufs=8))
+        epool = ctx.enter_context(tc.tile_pool(name="epool", bufs=6))
+        opool = ctx.enter_context(tc.tile_pool(name="opool", bufs=3))
+        psk = ctx.enter_context(tc.psum_pool(name="psk", bufs=2))
+        pss = ctx.enter_context(tc.psum_pool(name="pss", bufs=3))
+        pst = ctx.enter_context(tc.psum_pool(name="pst", bufs=3))
+
+        bias_bf = const.tile([P, PACK], BF16, name="bias_bf")
+        nc.scalar.dma_start(out=bias_bf[:], in_=bk_dr.rearrange("(p t) -> p t", t=PACK))
+        w_raw = const.tile([P, PACK * C], BF16, name="w_raw")
+        nc.sync.dma_start(out=w_raw[:], in_=Wk_dr.rearrange("(p t) c -> p (t c)", t=PACK))
+        seg_raw = []
+        q_raw = []
+        for b in range(B):
+            sr = raw.tile([P, PACK * N], BF16, name="seg_raw%d" % b)
+            nc.sync.dma_start(out=sr[:], in_=irSegF[b].rearrange("(p t) h w -> p (t h w)", t=PACK))
+            seg_raw.append(sr)
+            qr = raw.tile([P, PACK * N], BF16, name="q_raw%d" % b)
+            nc.sync.dma_start(out=qr[:], in_=q_ir[b].rearrange("(p t) n -> p (t n)", t=PACK))
+            q_raw.append(qr)
+
+        warm_in = const.tile([P, 1], F32, name="warm_in")
+        warm_out = const.tile([P, 1], F32, name="warm_out")
+        nc.vector.memset(warm_in[:], 0.0)
+        nc.scalar.activation(out=warm_out[:], in_=warm_in[:], func=ACT.Exp)
+        ident = const.tile([P, P], F32, name="ident")
+        make_identity(nc, ident[:])
+        bias_f = const.tile([P, PACK], F32, name="bias_f")
+        nc.vector.tensor_copy(out=bias_f[:], in_=bias_bf[:])
+
+        w_words = w_raw[:].bitcast(F32).rearrange("p (t w u) -> p t u w", t=PACK, u=2)
+        w_grp = const.tile([P, PACK * C], BF16, name="w_grp", align_bytes=64)
+        w_grp_f = w_grp[:].bitcast(F32)
+        for h in range(2):
+            wt = pst.tile([P, 512], F32, name="wt", tag="tp")
+            for t2 in range(2):
+                for u in range(2):
+                    nc.tensor.transpose(
+                        wt[:, (t2 * 2 + u) * P : (t2 * 2 + u + 1) * P], w_words[:, 2 * h + t2, u, :], ident[:]
+                    )
+            dst = w_grp_f[:, h * 512 : (h + 1) * 512].rearrange("p (t c u) -> p t c u", t=2, u=2)
+            src = wt[:].rearrange("p (t u c) -> p t c u", t=2, u=2)
+            if h == 0:
+                nc.vector.tensor_copy(out=dst, in_=src)
+            else:
+                nc.scalar.copy(out=dst, in_=src)
+        w_code = const.tile([P, C], U32, name="w_code", align_bytes=64)
+        w_scale = const.tile([P, C], U8, name="w_scale", align_bytes=64)
+        nc.vector.quantize_mx(out=w_code[:].bitcast(FP8X4), scales=w_scale[:], in_=w_grp[:])
+
+        def regroup(src_tile, dst_tile, s_cols):
+            for eng, c0, c1 in (("s", 0, s_cols), ("v", s_cols, N)):
+                if c1 <= c0:
+                    continue
+                dst = dst_tile[:, c0 * PACK : c1 * PACK].rearrange("p (c i t) -> p c t i", i=4, t=PACK)
+                src = src_tile[:].rearrange("p (t n) -> p t n", t=PACK)[:, :, c0:c1].rearrange(
+                    "p t (c i) -> p c t i", i=4
+                )
+                if eng == "s":
+                    nc.scalar.copy(out=dst, in_=src)
+                else:
+                    nc.vector.tensor_copy(out=dst, in_=src)
+
+        def quantise(grouped, tag):
+            code = wrd.tile([P, N], U32, name=tag + "_code", align_bytes=64)
+            scale = wrd.tile([P, N], U8, name=tag + "_scale", align_bytes=64)
+            nc.vector.quantize_mx(out=code[:].bitcast(FP8X4), scales=scale[:], in_=grouped[:])
+            return code, scale
+
+        bias_bc = bias_f[:].unsqueeze(1).to_broadcast([P, P, PACK])
+
+        for b in range(B):
+            seg_g = grp.tile([P, PACK * N], BF16, name="seg_g", align_bytes=64)
+            regroup(seg_raw[b], seg_g, SEG_S[b])
+            q_g = grp.tile([P, PACK * N], BF16, name="q_g", align_bytes=64)
+            regroup(q_raw[b], q_g, Q_S[b])
+            seg_code, seg_scale = quantise(seg_g, "seg")
+            key_g = grp.tile([P, PACK * N], BF16, name="key_g", align_bytes=64)
+            for j in range(4):
+                cols = slice(j * P, (j + 1) * P)
+                kp = psk.tile([P, 512], F32, name="kp")
+                for t in range(PACK):
+                    nc.tensor.matmul_mx(
+                        out=kp[:, t * P : (t + 1) * P],
+                        lhsT=w_code[:, t * P : (t + 1) * P].bitcast(FP8X4),
+                        lhsT_scale=w_scale[:, t * P : (t + 1) * P],
+                        rhs=seg_code[:, cols].bitcast(FP8X4),
+                        rhs_scale=seg_scale[:, cols],
+                        start=True,
+                        stop=True,
+                    )
+                nc.vector.tensor_tensor(
+                    out=key_g[:, j * 512 : (j + 1) * 512].rearrange("p (m t) -> p m t", t=PACK),
+                    in0=kp[:].rearrange("p (t m) -> p m t", t=PACK),
+                    in1=bias_bc,
+                    op=ALU.add,
+                )
+            q_code, q_scale = quantise(q_g, "q")
+            key_code, key_scale = quantise(key_g, "key")
+            ot = opool.tile([P, 4, N], F32, name="ot")
+            for j in range(4):
+                u = 4 * b + j
+                cols = slice(j * P, (j + 1) * P)
+                sp = pss.tile([P, 512], F32, name="sp")
+                nc.tensor.matmul_mx(
+                    out=sp[:],
+                    lhsT=key_code[:, cols].bitcast(FP8X4),
+                    lhsT_scale=key_scale[:, cols],
+                    rhs=q_code[:].bitcast(FP8X4),
+                    rhs_scale=q_scale[:],
+                    start=True,
+                    stop=True,
+                )
+                nmax = stat.tile([P, 1], F32, name="nmax")
+                nc.vector.tensor_reduce(out=nmax[:], in_=sp[:], axis=AX.X, op=ALU.max, negate=True)
+                e = epool.tile([P, N], F32, name="e")
+                ssum = stat.tile([P, 1], F32, name="ssum")
+                nc.scalar.activation(out=e[:], in_=sp[:], func=ACT.Exp, bias=nmax[:], scale=1.0, accum_out=ssum[:])
+                rsum = stat.tile([P, 1], F32, name="rsum")
+                nc.vector.reciprocal(out=rsum[:], in_=ssum[:])
+                en = epool.tile([P, N], F32, name="en")
+                if u in NORM_V:
+                    nc.vector.tensor_scalar_mul(out=en[:], in0=e[:], scalar1=rsum[:])
+                else:
+                    nc.scalar.activation(out=en[:], in_=e[:], func=ACT.Copy, scale=rsum[:])
+                tp = pst.tile([P, 512], F32, name="tp")
+                for i in range(4):
+                    nc.tensor.transpose(tp[:, i * P : (i + 1) * P], en[:, i * P : (i + 1) * P], ident[:])
+                dst = ot[:, :, cols]
+                src = tp[:].rearrange("p (i m) -> p i m", i=4)
+                if u in EVAC_V:
+                    nc.vector.tensor_copy(out=dst, in_=src)
+                else:
+                    nc.scalar.copy(out=dst, in_=src)
+            nc.sync.dma_start(out=out[b].rearrange("(i p) m -> p i m", p=P), in_=ot[:])

@@ -1,8 +1,6 @@
 from contextlib import ExitStack
 
-import concourse.bass as bass
 import concourse.mybir as mybir
-import concourse.tile as tile
 from concourse.masks import make_identity
 
 F32 = mybir.dt.float32
@@ -19,12 +17,11 @@ B = 8
 C = 512
 N = 512
 PACK = 4
+UNITS = 4 * B
 FLOPS = 2 * 2 * B * C * N * N
 
-SEG_S = [128, 512, 0, 384, 128, 128, 0, 128]
-Q_S = [384, 512, 256, 128, 128, 128, 256, 0]
-NORM_V = [26, 28, 29, 30, 31]
-EVAC_V = [29, 31]
+SEG_S_COLS = 128
+FIRST_LATE_UNIT = UNITS - 8
 
 
 def tile_featuremaptransformer_pb_t_kernel(tc, q_ir, irSegF, Wk_dr, bk_dr, out):
@@ -35,11 +32,12 @@ def tile_featuremaptransformer_pb_t_kernel(tc, q_ir, irSegF, Wk_dr, bk_dr, out):
         grp = ctx.enter_context(tc.tile_pool(name="grp", bufs=3))
         wrd = ctx.enter_context(tc.tile_pool(name="wrd", bufs=3))
         stat = ctx.enter_context(tc.tile_pool(name="stat", bufs=8))
-        epool = ctx.enter_context(tc.tile_pool(name="epool", bufs=6))
+        epool = ctx.enter_context(tc.tile_pool(name="epool", bufs=4))
         opool = ctx.enter_context(tc.tile_pool(name="opool", bufs=3))
         psk = ctx.enter_context(tc.psum_pool(name="psk", bufs=2))
         pss = ctx.enter_context(tc.psum_pool(name="pss", bufs=3))
         pst = ctx.enter_context(tc.psum_pool(name="pst", bufs=3))
+        ctx.enter_context(tc.manual_schedule())
 
         bias_bf = const.tile([P, PACK], BF16, name="bias_bf")
         nc.scalar.dma_start(out=bias_bf[:], in_=bk_dr.rearrange("(p t) -> p t", t=PACK))
@@ -62,20 +60,149 @@ def tile_featuremaptransformer_pb_t_kernel(tc, q_ir, irSegF, Wk_dr, bk_dr, out):
         ident = const.tile([P, P], F32, name="ident")
         make_identity(nc, ident[:])
         bias_f = const.tile([P, PACK], F32, name="bias_f")
-        nc.vector.tensor_copy(out=bias_f[:], in_=bias_bf[:])
+        bias_bc = bias_f[:].unsqueeze(1).to_broadcast([P, P, PACK])
+
+        seg_g, q_g, key_g = {}, {}, {}
+        seg_mx, q_mx, key_mx = {}, {}, {}
+        kp, sp, tp = {}, {}, {}
+        nmax, ssum, rsum, e, en, ot = {}, {}, {}, {}, {}, {}
+
+        def grouped(store, b, name):
+            if b not in store:
+                store[b] = grp.tile([P, PACK * N], BF16, name=name, align_bytes=64)
+            return store[b]
+
+        def regroup(engine, src_tile, dst_tile, c0, c1):
+            dst = dst_tile[:, c0 * PACK : c1 * PACK].rearrange("p (c i t) -> p c t i", i=4, t=PACK)
+            src = src_tile[:].rearrange("p (t n) -> p t n", t=PACK)[:, :, c0:c1].rearrange("p t (c i) -> p c t i", i=4)
+            if engine == "scalar":
+                nc.scalar.copy(out=dst, in_=src)
+            else:
+                nc.vector.tensor_copy(out=dst, in_=src)
+
+        def regroup_seg(engine, b):
+            if 0 <= b < B:
+                if engine == "scalar":
+                    regroup(engine, seg_raw[b], grouped(seg_g, b, "seg_g"), 0, SEG_S_COLS)
+                else:
+                    regroup(engine, seg_raw[b], grouped(seg_g, b, "seg_g"), SEG_S_COLS, N)
+
+        def regroup_q(b, j):
+            if 0 <= b < B:
+                regroup("scalar", q_raw[b], grouped(q_g, b, "q_g"), j * P, (j + 1) * P)
+
+        def quantise(src, dst, b, name):
+            if 0 <= b < B:
+                code = wrd.tile([P, N], U32, name=name + "_code", align_bytes=64)
+                scale = wrd.tile([P, N], U8, name=name + "_scale", align_bytes=64)
+                nc.vector.quantize_mx(out=code[:].bitcast(FP8X4), scales=scale[:], in_=src[b][:])
+                dst[b] = (code, scale)
+
+        def key_matmul(u):
+            if 0 <= u < UNITS:
+                code, scale = seg_mx[u // 4]
+                cols = slice((u % 4) * P, (u % 4 + 1) * P)
+                kp[u] = psk.tile([P, 512], F32, name="kp")
+                for t in range(PACK):
+                    nc.tensor.matmul_mx(
+                        out=kp[u][:, t * P : (t + 1) * P],
+                        lhsT=w_code[:, t * P : (t + 1) * P].bitcast(FP8X4),
+                        lhsT_scale=w_scale[:, t * P : (t + 1) * P],
+                        rhs=code[:, cols].bitcast(FP8X4),
+                        rhs_scale=scale[:, cols],
+                        start=True,
+                        stop=True,
+                    )
+
+        def key_out(u):
+            if 0 <= u < UNITS:
+                dst = grouped(key_g, u // 4, "key_g")
+                nc.vector.tensor_tensor(
+                    out=dst[:, (u % 4) * 512 : (u % 4 + 1) * 512].rearrange("p (m t) -> p m t", t=PACK),
+                    in0=kp[u][:].rearrange("p (t m) -> p m t", t=PACK),
+                    in1=bias_bc,
+                    op=ALU.add,
+                )
+
+        def score_matmul(u):
+            if 0 <= u < UNITS:
+                k_code, k_scale = key_mx[u // 4]
+                q_code, q_scale = q_mx[u // 4]
+                cols = slice((u % 4) * P, (u % 4 + 1) * P)
+                sp[u] = pss.tile([P, 512], F32, name="sp")
+                nc.tensor.matmul_mx(
+                    out=sp[u][:],
+                    lhsT=k_code[:, cols].bitcast(FP8X4),
+                    lhsT_scale=k_scale[:, cols],
+                    rhs=q_code[:].bitcast(FP8X4),
+                    rhs_scale=q_scale[:],
+                    start=True,
+                    stop=True,
+                )
+
+        def row_max(u):
+            if 0 <= u < UNITS:
+                nmax[u] = stat.tile([P, 1], F32, name="nmax")
+                nc.vector.tensor_reduce(out=nmax[u][:], in_=sp[u][:], axis=AX.X, op=ALU.max, negate=True)
+
+        def exponent(u):
+            if 0 <= u < UNITS:
+                e[u] = epool.tile([P, N], F32, name="e")
+                ssum[u] = stat.tile([P, 1], F32, name="ssum")
+                nc.scalar.activation(
+                    out=e[u][:], in_=sp[u][:], func=ACT.Exp, bias=nmax[u][:], scale=1.0, accum_out=ssum[u][:]
+                )
+
+        def reciprocal(u):
+            if 0 <= u < UNITS:
+                rsum[u] = stat.tile([P, 1], F32, name="rsum")
+                nc.vector.reciprocal(out=rsum[u][:], in_=ssum[u][:])
+
+        def normalise(engine, u):
+            if 0 <= u < UNITS:
+                en[u] = epool.tile([P, N], F32, name="en")
+                if engine == "vector":
+                    nc.vector.tensor_scalar_mul(out=en[u][:], in0=e[u][:], scalar1=rsum[u][:])
+                else:
+                    nc.gpsimd.tensor_scalar(
+                        out=en[u][:], in0=e[u][:], scalar1=rsum[u][:], scalar2=0.0, op0=ALU.mult, op1=ALU.add
+                    )
+
+        def transposes(u):
+            if 0 <= u < UNITS:
+                tp[u] = pst.tile([P, 512], F32, name="tp")
+                for i in range(4):
+                    nc.tensor.transpose(tp[u][:, i * P : (i + 1) * P], en[u][:, i * P : (i + 1) * P], ident[:])
+
+        def out_copy_and_store(u):
+            if 0 <= u < UNITS:
+                b = u // 4
+                cols = slice((u % 4) * P, (u % 4 + 1) * P)
+                if u % 4 == 0:
+                    ot[b] = opool.tile([P, 4, N], F32, name="ot")
+                nc.scalar.copy(out=ot[b][:, :, cols], in_=tp[u][:].rearrange("p (i m) -> p i m", i=4))
+                rows = out[b].rearrange("(i p) m -> p i m", p=P)
+                if b == B - 1:
+                    nc.sync.dma_start(out=rows[:, :, cols], in_=ot[b][:, :, cols])
+                elif u % 4 == 3:
+                    nc.sync.dma_start(out=rows, in_=ot[b][:])
 
         w_words = w_raw[:].bitcast(F32).rearrange("p (t w u) -> p t u w", t=PACK, u=2)
         w_grp = const.tile([P, PACK * C], BF16, name="w_grp", align_bytes=64)
         w_grp_f = w_grp[:].bitcast(F32)
+        wt = []
         for h in range(2):
-            wt = pst.tile([P, 512], F32, name="wt", tag="tp")
+            wt.append(pst.tile([P, 512], F32, name="wt", tag="tp"))
             for t2 in range(2):
-                for u in range(2):
+                for u2 in range(2):
                     nc.tensor.transpose(
-                        wt[:, (t2 * 2 + u) * P : (t2 * 2 + u + 1) * P], w_words[:, 2 * h + t2, u, :], ident[:]
+                        wt[h][:, (t2 * 2 + u2) * P : (t2 * 2 + u2 + 1) * P], w_words[:, 2 * h + t2, u2, :], ident[:]
                     )
+        regroup_seg("scalar", 0)
+        regroup_seg("vector", 0)
+        for h in range(2):
             dst = w_grp_f[:, h * 512 : (h + 1) * 512].rearrange("p (t c u) -> p t c u", t=2, u=2)
-            src = wt[:].rearrange("p (t u c) -> p t c u", t=2, u=2)
+            src = wt[h][:].rearrange("p (t u c) -> p t c u", t=2, u=2)
             if h == 0:
                 nc.vector.tensor_copy(out=dst, in_=src)
             else:
@@ -83,89 +210,33 @@ def tile_featuremaptransformer_pb_t_kernel(tc, q_ir, irSegF, Wk_dr, bk_dr, out):
         w_code = const.tile([P, C], U32, name="w_code", align_bytes=64)
         w_scale = const.tile([P, C], U8, name="w_scale", align_bytes=64)
         nc.vector.quantize_mx(out=w_code[:].bitcast(FP8X4), scales=w_scale[:], in_=w_grp[:])
+        nc.vector.tensor_copy(out=bias_f[:], in_=bias_bf[:])
 
-        def regroup(src_tile, dst_tile, s_cols):
-            for eng, c0, c1 in (("s", 0, s_cols), ("v", s_cols, N)):
-                if c1 <= c0:
-                    continue
-                dst = dst_tile[:, c0 * PACK : c1 * PACK].rearrange("p (c i t) -> p c t i", i=4, t=PACK)
-                src = src_tile[:].rearrange("p (t n) -> p t n", t=PACK)[:, :, c0:c1].rearrange(
-                    "p t (c i) -> p c t i", i=4
-                )
-                if eng == "s":
-                    nc.scalar.copy(out=dst, in_=src)
-                else:
-                    nc.vector.tensor_copy(out=dst, in_=src)
-
-        def quantise(grouped, tag):
-            code = wrd.tile([P, N], U32, name=tag + "_code", align_bytes=64)
-            scale = wrd.tile([P, N], U8, name=tag + "_scale", align_bytes=64)
-            nc.vector.quantize_mx(out=code[:].bitcast(FP8X4), scales=scale[:], in_=grouped[:])
-            return code, scale
-
-        bias_bc = bias_f[:].unsqueeze(1).to_broadcast([P, P, PACK])
-
-        for b in range(B):
-            seg_g = grp.tile([P, PACK * N], BF16, name="seg_g", align_bytes=64)
-            regroup(seg_raw[b], seg_g, SEG_S[b])
-            q_g = grp.tile([P, PACK * N], BF16, name="q_g", align_bytes=64)
-            regroup(q_raw[b], q_g, Q_S[b])
-            seg_code, seg_scale = quantise(seg_g, "seg")
-            key_g = grp.tile([P, PACK * N], BF16, name="key_g", align_bytes=64)
-            for j in range(4):
-                cols = slice(j * P, (j + 1) * P)
-                kp = psk.tile([P, 512], F32, name="kp")
-                for t in range(PACK):
-                    nc.tensor.matmul_mx(
-                        out=kp[:, t * P : (t + 1) * P],
-                        lhsT=w_code[:, t * P : (t + 1) * P].bitcast(FP8X4),
-                        lhsT_scale=w_scale[:, t * P : (t + 1) * P],
-                        rhs=seg_code[:, cols].bitcast(FP8X4),
-                        rhs_scale=seg_scale[:, cols],
-                        start=True,
-                        stop=True,
-                    )
-                nc.vector.tensor_tensor(
-                    out=key_g[:, j * 512 : (j + 1) * 512].rearrange("p (m t) -> p m t", t=PACK),
-                    in0=kp[:].rearrange("p (t m) -> p m t", t=PACK),
-                    in1=bias_bc,
-                    op=ALU.add,
-                )
-            q_code, q_scale = quantise(q_g, "q")
-            key_code, key_scale = quantise(key_g, "key")
-            ot = opool.tile([P, 4, N], F32, name="ot")
-            for j in range(4):
-                u = 4 * b + j
-                cols = slice(j * P, (j + 1) * P)
-                sp = pss.tile([P, 512], F32, name="sp")
-                nc.tensor.matmul_mx(
-                    out=sp[:],
-                    lhsT=key_code[:, cols].bitcast(FP8X4),
-                    lhsT_scale=key_scale[:, cols],
-                    rhs=q_code[:].bitcast(FP8X4),
-                    rhs_scale=q_scale[:],
-                    start=True,
-                    stop=True,
-                )
-                nmax = stat.tile([P, 1], F32, name="nmax")
-                nc.vector.tensor_reduce(out=nmax[:], in_=sp[:], axis=AX.X, op=ALU.max, negate=True)
-                e = epool.tile([P, N], F32, name="e")
-                ssum = stat.tile([P, 1], F32, name="ssum")
-                nc.scalar.activation(out=e[:], in_=sp[:], func=ACT.Exp, bias=nmax[:], scale=1.0, accum_out=ssum[:])
-                rsum = stat.tile([P, 1], F32, name="rsum")
-                nc.vector.reciprocal(out=rsum[:], in_=ssum[:])
-                en = epool.tile([P, N], F32, name="en")
-                if u in NORM_V:
-                    nc.vector.tensor_scalar_mul(out=en[:], in0=e[:], scalar1=rsum[:])
-                else:
-                    nc.scalar.activation(out=en[:], in_=e[:], func=ACT.Copy, scale=rsum[:])
-                tp = pst.tile([P, 512], F32, name="tp")
-                for i in range(4):
-                    nc.tensor.transpose(tp[:, i * P : (i + 1) * P], en[:, i * P : (i + 1) * P], ident[:])
-                dst = ot[:, :, cols]
-                src = tp[:].rearrange("p (i m) -> p i m", i=4)
-                if u in EVAC_V:
-                    nc.vector.tensor_copy(out=dst, in_=src)
-                else:
-                    nc.scalar.copy(out=dst, in_=src)
-            nc.sync.dma_start(out=out[b].rearrange("(i p) m -> p i m", p=P), in_=ot[:])
+        for s in range(-12, UNITS + 3):
+            b, j = s // 4, s % 4
+            if j == 0 and b + 2 > 0:
+                regroup_seg("vector", b + 2)
+            if j == 1:
+                quantise(seg_g, seg_mx, b + 2, "seg")
+            if j == 2:
+                quantise(key_g, key_mx, b + 1, "key")
+            if j == 3:
+                quantise(q_g, q_mx, b + 2, "q")
+            late = s - 1 >= FIRST_LATE_UNIT
+            if not late:
+                reciprocal(s - 1)
+            row_max(s)
+            if late:
+                reciprocal(s - 1)
+                normalise("vector", s - 1)
+            key_out(s + 6)
+            if not late:
+                normalise("gpsimd", s - 1)
+            exponent(s)
+            out_copy_and_store(s - 2)
+            if j == 0 and b + 3 > 0:
+                regroup_seg("scalar", b + 3)
+            regroup_q(b + 3, j)
+            key_matmul(s + 7)
+            score_matmul(s + 1)
+            transposes(s - 1)

@@ -59,6 +59,8 @@ def tile_featuremaptransformer_pb_t_kernel(tc, q_ir, irSegF, Wk_dr, bk_dr, out):
         nc.scalar.activation(out=warm_out[:], in_=warm_in[:], func=ACT.Exp)
         ident = const.tile([P, P], F32, name="ident")
         make_identity(nc, ident[:])
+        minus_one = const.tile([P, 1], F32, name="minus_one")
+        nc.gpsimd.memset(minus_one[:], -1.0)
         bias_f = const.tile([P, PACK], F32, name="bias_f")
         bias_bc = bias_f[:].unsqueeze(1).to_broadcast([P, P, PACK])
 
@@ -153,10 +155,13 @@ def tile_featuremaptransformer_pb_t_kernel(tc, q_ir, irSegF, Wk_dr, bk_dr, out):
                     out=e[u][:], in_=sp[u][:], func=ACT.Exp, bias=nmax[u][:], scale=1.0, accum_out=ssum[u][:]
                 )
 
-        def reciprocal(u):
+        def reciprocal(engine, u):
             if 0 <= u < UNITS:
                 rsum[u] = stat.tile([P, 1], F32, name="rsum")
-                nc.vector.reciprocal(out=rsum[u][:], in_=ssum[u][:])
+                if engine == "vector":
+                    nc.vector.reciprocal(out=rsum[u][:], in_=ssum[u][:])
+                else:
+                    nc.gpsimd.tensor_tensor(out=rsum[u][:], in0=ssum[u][:], in1=minus_one[:], op=ALU.pow)
 
         def normalise(engine, u):
             if 0 <= u < UNITS:
@@ -223,14 +228,13 @@ def tile_featuremaptransformer_pb_t_kernel(tc, q_ir, irSegF, Wk_dr, bk_dr, out):
             if j == 3:
                 quantise(q_g, q_mx, b + 2, "q")
             late = s - 1 >= FIRST_LATE_UNIT
-            if not late:
-                reciprocal(s - 1)
             row_max(s)
             if late:
-                reciprocal(s - 1)
+                reciprocal("vector", s - 1)
                 normalise("vector", s - 1)
             key_out(s + 6)
             if not late:
+                reciprocal("gpsimd", s - 1)
                 normalise("gpsimd", s - 1)
             exponent(s)
             out_copy_and_store(s - 2)

@@ -21,7 +21,8 @@ UNITS = 4 * B
 FLOPS = 2 * 2 * B * C * N * N
 
 SEG_S_COLS = 128
-FIRST_LATE_UNIT = UNITS - 8
+SEG_V_HALF = (N - SEG_S_COLS) // 2
+FIRST_LATE_UNIT = UNITS - 4
 
 
 def tile_featuremaptransformer_pb_t_kernel(tc, q_ir, irSegF, Wk_dr, bk_dr, out):
@@ -31,6 +32,7 @@ def tile_featuremaptransformer_pb_t_kernel(tc, q_ir, irSegF, Wk_dr, bk_dr, out):
         raw = ctx.enter_context(tc.tile_pool(name="raw", bufs=1))
         grp = ctx.enter_context(tc.tile_pool(name="grp", bufs=3))
         wrd = ctx.enter_context(tc.tile_pool(name="wrd", bufs=3))
+        keyp = ctx.enter_context(tc.tile_pool(name="keyp", bufs=4))
         stat = ctx.enter_context(tc.tile_pool(name="stat", bufs=8))
         epool = ctx.enter_context(tc.tile_pool(name="epool", bufs=4))
         opool = ctx.enter_context(tc.tile_pool(name="opool", bufs=3))
@@ -59,8 +61,6 @@ def tile_featuremaptransformer_pb_t_kernel(tc, q_ir, irSegF, Wk_dr, bk_dr, out):
         nc.scalar.activation(out=warm_out[:], in_=warm_in[:], func=ACT.Exp)
         ident = const.tile([P, P], F32, name="ident")
         make_identity(nc, ident[:])
-        minus_one = const.tile([P, 1], F32, name="minus_one")
-        nc.gpsimd.memset(minus_one[:], -1.0)
         bias_f = const.tile([P, PACK], F32, name="bias_f")
         bias_bc = bias_f[:].unsqueeze(1).to_broadcast([P, P, PACK])
 
@@ -82,16 +82,18 @@ def tile_featuremaptransformer_pb_t_kernel(tc, q_ir, irSegF, Wk_dr, bk_dr, out):
             else:
                 nc.vector.tensor_copy(out=dst, in_=src)
 
-        def regroup_seg(engine, b):
+        def regroup_seg(part, b):
             if 0 <= b < B:
-                if engine == "scalar":
-                    regroup(engine, seg_raw[b], grouped(seg_g, b, "seg_g"), 0, SEG_S_COLS)
+                dst = grouped(seg_g, b, "seg_g")
+                if part == 0:
+                    regroup("scalar", seg_raw[b], dst, 0, SEG_S_COLS)
                 else:
-                    regroup(engine, seg_raw[b], grouped(seg_g, b, "seg_g"), SEG_S_COLS, N)
+                    c0 = SEG_S_COLS + (part - 1) * SEG_V_HALF
+                    regroup("vector", seg_raw[b], dst, c0, c0 + SEG_V_HALF)
 
-        def regroup_q(b, j):
-            if 0 <= b < B:
-                regroup("scalar", q_raw[b], grouped(q_g, b, "q_g"), j * P, (j + 1) * P)
+        def regroup_q(k):
+            if 0 <= k < UNITS:
+                regroup("scalar", q_raw[k // 4], grouped(q_g, k // 4, "q_g"), (k % 4) * P, (k % 4 + 1) * P)
 
         def quantise(src, dst, b, name):
             if 0 <= b < B:
@@ -118,24 +120,30 @@ def tile_featuremaptransformer_pb_t_kernel(tc, q_ir, irSegF, Wk_dr, bk_dr, out):
 
         def key_out(u):
             if 0 <= u < UNITS:
-                dst = grouped(key_g, u // 4, "key_g")
+                key_g[u] = keyp.tile([P, PACK * P], BF16, name="key_g", align_bytes=64)
                 nc.vector.tensor_tensor(
-                    out=dst[:, (u % 4) * 512 : (u % 4 + 1) * 512].rearrange("p (m t) -> p m t", t=PACK),
+                    out=key_g[u][:].rearrange("p (m t) -> p m t", t=PACK),
                     in0=kp[u][:].rearrange("p (t m) -> p m t", t=PACK),
                     in1=bias_bc,
                     op=ALU.add,
                 )
 
+        def quantise_key(u):
+            if 0 <= u < UNITS:
+                code = keyp.tile([P, P], U32, name="key_code", align_bytes=64)
+                scale = keyp.tile([P, P], U8, name="key_scale", align_bytes=64)
+                nc.vector.quantize_mx(out=code[:].bitcast(FP8X4), scales=scale[:], in_=key_g[u][:])
+                key_mx[u] = (code, scale)
+
         def score_matmul(u):
             if 0 <= u < UNITS:
-                k_code, k_scale = key_mx[u // 4]
+                k_code, k_scale = key_mx[u]
                 q_code, q_scale = q_mx[u // 4]
-                cols = slice((u % 4) * P, (u % 4 + 1) * P)
                 sp[u] = pss.tile([P, 512], F32, name="sp")
                 nc.tensor.matmul_mx(
                     out=sp[u][:],
-                    lhsT=k_code[:, cols].bitcast(FP8X4),
-                    lhsT_scale=k_scale[:, cols],
+                    lhsT=k_code[:].bitcast(FP8X4),
+                    lhsT_scale=k_scale[:],
                     rhs=q_code[:].bitcast(FP8X4),
                     rhs_scale=q_scale[:],
                     start=True,
@@ -155,13 +163,10 @@ def tile_featuremaptransformer_pb_t_kernel(tc, q_ir, irSegF, Wk_dr, bk_dr, out):
                     out=e[u][:], in_=sp[u][:], func=ACT.Exp, bias=nmax[u][:], scale=1.0, accum_out=ssum[u][:]
                 )
 
-        def reciprocal(engine, u):
+        def reciprocal(u):
             if 0 <= u < UNITS:
                 rsum[u] = stat.tile([P, 1], F32, name="rsum")
-                if engine == "vector":
-                    nc.vector.reciprocal(out=rsum[u][:], in_=ssum[u][:])
-                else:
-                    nc.gpsimd.tensor_tensor(out=rsum[u][:], in0=ssum[u][:], in1=minus_one[:], op=ALU.pow)
+                nc.vector.reciprocal(out=rsum[u][:], in_=ssum[u][:])
 
         def normalise(engine, u):
             if 0 <= u < UNITS:
@@ -203,8 +208,8 @@ def tile_featuremaptransformer_pb_t_kernel(tc, q_ir, irSegF, Wk_dr, bk_dr, out):
                     nc.tensor.transpose(
                         wt[h][:, (t2 * 2 + u2) * P : (t2 * 2 + u2 + 1) * P], w_words[:, 2 * h + t2, u2, :], ident[:]
                     )
-        regroup_seg("scalar", 0)
-        regroup_seg("vector", 0)
+        for part in range(3):
+            regroup_seg(part, 0)
         for h in range(2):
             dst = w_grp_f[:, h * 512 : (h + 1) * 512].rearrange("p (t c u) -> p t c u", t=2, u=2)
             src = wt[h][:].rearrange("p (t u c) -> p t c u", t=2, u=2)
@@ -217,30 +222,32 @@ def tile_featuremaptransformer_pb_t_kernel(tc, q_ir, irSegF, Wk_dr, bk_dr, out):
         nc.vector.quantize_mx(out=w_code[:].bitcast(FP8X4), scales=w_scale[:], in_=w_grp[:])
         nc.vector.tensor_copy(out=bias_f[:], in_=bias_bf[:])
 
-        for s in range(-12, UNITS + 3):
+        for s in range(-8, UNITS + 3):
             b, j = s // 4, s % 4
-            if j == 0 and b + 2 > 0:
-                regroup_seg("vector", b + 2)
-            if j == 1:
-                quantise(seg_g, seg_mx, b + 2, "seg")
+            if j == 0:
+                quantise(seg_g, seg_mx, b + 1, "seg")
+            if j == 1 and b + 2 > 0:
+                regroup_seg(1, b + 2)
             if j == 2:
-                quantise(key_g, key_mx, b + 1, "key")
-            if j == 3:
-                quantise(q_g, q_mx, b + 2, "q")
+                quantise(q_g, q_mx, b + 1, "q")
+            if j == 3 and b + 2 > 0:
+                regroup_seg(2, b + 2)
+            quantise_key(s + 1)
             late = s - 1 >= FIRST_LATE_UNIT
+            if not late:
+                reciprocal(s - 1)
             row_max(s)
             if late:
-                reciprocal("vector", s - 1)
+                reciprocal(s - 1)
                 normalise("vector", s - 1)
-            key_out(s + 6)
+            key_out(s + 2)
             if not late:
-                reciprocal("gpsimd", s - 1)
                 normalise("gpsimd", s - 1)
             exponent(s)
             out_copy_and_store(s - 2)
-            if j == 0 and b + 3 > 0:
-                regroup_seg("scalar", b + 3)
-            regroup_q(b + 3, j)
-            key_matmul(s + 7)
+            if j == 2 and b + 2 > 0:
+                regroup_seg(0, b + 2)
+            regroup_q(s + 8)
+            key_matmul(s + 3)
             score_matmul(s + 1)
             transposes(s - 1)

@@ -44,7 +44,9 @@ def tile_featuremaptransformer_pb_t_kernel(tc, q_ir, irSegF, Wk_dr, bk_dr, out):
         bias_bf = const.tile([P, PACK], BF16, name="bias_bf")
         nc.scalar.dma_start(out=bias_bf[:], in_=bk_dr.rearrange("(p t) -> p t", t=PACK))
         w_raw = const.tile([P, PACK * C], BF16, name="w_raw")
-        nc.sync.dma_start(out=w_raw[:], in_=Wk_dr.rearrange("(p t) c -> p (t c)", t=PACK))
+        w_rows = Wk_dr.rearrange("(p t) c -> p (t c)", t=PACK)
+        for h in range(2):
+            nc.sync.dma_start(out=w_raw[:, h * 2 * C : (h + 1) * 2 * C], in_=w_rows[:, h * 2 * C : (h + 1) * 2 * C])
         seg_raw = []
         q_raw = []
         for b in range(B):
@@ -192,7 +194,7 @@ def tile_featuremaptransformer_pb_t_kernel(tc, q_ir, irSegF, Wk_dr, bk_dr, out):
                     ot[b] = opool.tile([P, 4, N], F32, name="ot")
                 nc.scalar.copy(out=ot[b][:, :, cols], in_=tp[u][:].rearrange("p (i m) -> p i m", i=4))
                 rows = out[b].rearrange("(i p) m -> p i m", p=P)
-                if b == B - 1:
+                if b >= B - 2:
                     nc.sync.dma_start(out=rows[:, :, cols], in_=ot[b][:, :, cols])
                 elif u % 4 == 3:
                     nc.sync.dma_start(out=rows, in_=ot[b][:])
@@ -208,22 +210,20 @@ def tile_featuremaptransformer_pb_t_kernel(tc, q_ir, irSegF, Wk_dr, bk_dr, out):
                     nc.tensor.transpose(
                         wt[h][:, (t2 * 2 + u2) * P : (t2 * 2 + u2 + 1) * P], w_words[:, 2 * h + t2, u2, :], ident[:]
                     )
-        for part in range(3):
-            regroup_seg(part, 0)
         for h in range(2):
             dst = w_grp_f[:, h * 512 : (h + 1) * 512].rearrange("p (t c u) -> p t c u", t=2, u=2)
             src = wt[h][:].rearrange("p (t u c) -> p t c u", t=2, u=2)
-            if h == 0:
-                nc.vector.tensor_copy(out=dst, in_=src)
-            else:
-                nc.scalar.copy(out=dst, in_=src)
+            nc.scalar.copy(out=dst, in_=src)
+        for part in range(3):
+            regroup_seg(part, 0)
         w_code = const.tile([P, C], U32, name="w_code", align_bytes=64)
         w_scale = const.tile([P, C], U8, name="w_scale", align_bytes=64)
         nc.vector.quantize_mx(out=w_code[:].bitcast(FP8X4), scales=w_scale[:], in_=w_grp[:])
         nc.vector.tensor_copy(out=bias_f[:], in_=bias_bf[:])
 
-        for s in range(-8, UNITS + 3):
-            b, j = s // 4, s % 4
+        for s in range(-9, UNITS + 3):
+            v = s + 1
+            b, j = v // 4, v % 4
             if j == 0:
                 quantise(seg_g, seg_mx, b + 1, "seg")
             if j == 1 and b + 2 > 0:
@@ -232,22 +232,22 @@ def tile_featuremaptransformer_pb_t_kernel(tc, q_ir, irSegF, Wk_dr, bk_dr, out):
                 quantise(q_g, q_mx, b + 1, "q")
             if j == 3 and b + 2 > 0:
                 regroup_seg(2, b + 2)
-            quantise_key(s + 1)
+            quantise_key(v + 1)
             late = s - 1 >= FIRST_LATE_UNIT
             if not late:
                 reciprocal(s - 1)
-            row_max(s)
+            row_max(v)
             if late:
                 reciprocal(s - 1)
                 normalise("vector", s - 1)
-            key_out(s + 2)
+            key_out(v + 2)
             if not late:
                 normalise("gpsimd", s - 1)
             exponent(s)
             out_copy_and_store(s - 2)
             if j == 2 and b + 2 > 0:
                 regroup_seg(0, b + 2)
-            regroup_q(s + 8)
-            key_matmul(s + 3)
-            score_matmul(s + 1)
+            regroup_q(v + 8)
+            key_matmul(v + 3)
+            score_matmul(v + 1)
             transposes(s - 1)

@@ -194,10 +194,7 @@ def tile_featuremaptransformer_pb_t_kernel(tc, q_ir, irSegF, Wk_dr, bk_dr, out):
                     ot[b] = opool.tile([P, 4, N], F32, name="ot")
                 nc.scalar.copy(out=ot[b][:, :, cols], in_=tp[u][:].rearrange("p (i m) -> p i m", i=4))
                 rows = out[b].rearrange("(i p) m -> p i m", p=P)
-                if b >= B - 2:
-                    nc.sync.dma_start(out=rows[:, :, cols], in_=ot[b][:, :, cols])
-                elif u % 4 == 3:
-                    nc.sync.dma_start(out=rows, in_=ot[b][:])
+                nc.sync.dma_start(out=rows[:, :, cols], in_=ot[b][:, :, cols])
 
         w_words = w_raw[:].bitcast(F32).rearrange("p (t w u) -> p t u w", t=PACK, u=2)
         w_grp = const.tile([P, PACK * C], BF16, name="w_grp", align_bytes=64)

@@ -22,6 +22,8 @@ FLOPS = 2 * 2 * B * C * N * N
 
 SEG_S_COLS = 128
 SEG_V_HALF = (N - SEG_S_COLS) // 2
+FIRST_POOL_BATCH = 3
+SEG_P_COLS = N // 8
 FIRST_LATE_UNIT = UNITS - 4
 
 
@@ -81,11 +83,20 @@ def tile_featuremaptransformer_pb_t_kernel(tc, q_ir, irSegF, Wk_dr, bk_dr, out):
             src = src_tile[:].rearrange("p (t n) -> p t n", t=PACK)[:, :, c0:c1].rearrange("p t (c i) -> p c t i", i=4)
             if engine == "scalar":
                 nc.scalar.copy(out=dst, in_=src)
+            elif engine == "gpsimd":
+                nc.gpsimd.tensor_scalar(out=dst, in0=src, scalar1=1.0, scalar2=0.0, op0=ALU.mult, op1=ALU.add)
             else:
                 nc.vector.tensor_copy(out=dst, in_=src)
 
+        def regroup_seg_pool(piece, b):
+            if FIRST_POOL_BATCH <= b < B:
+                regroup("gpsimd", seg_raw[b], grouped(seg_g, b, "seg_g"), piece * SEG_P_COLS, (piece + 1) * SEG_P_COLS)
+
         def regroup_seg(part, b):
-            if 0 <= b < B:
+            if FIRST_POOL_BATCH <= b < B and part > 0:
+                c0 = N // 2 + (part - 1) * N // 4
+                regroup("vector", seg_raw[b], grouped(seg_g, b, "seg_g"), c0, c0 + N // 4)
+            if 0 <= b < FIRST_POOL_BATCH:
                 dst = grouped(seg_g, b, "seg_g")
                 if part == 0:
                     regroup("scalar", seg_raw[b], dst, 0, SEG_S_COLS)
@@ -240,6 +251,7 @@ def tile_featuremaptransformer_pb_t_kernel(tc, q_ir, irSegF, Wk_dr, bk_dr, out):
             key_out(v + 2)
             if not late:
                 normalise("gpsimd", s - 1)
+            regroup_seg_pool((v + 10) % 4, (v + 10) // 4)
             exponent(s)
             out_copy_and_store(s - 2)
             if j == 2 and b + 2 > 0:

@@ -24,6 +24,9 @@ SEG_S_COLS = 128
 SEG_V_HALF = (N - SEG_S_COLS) // 2
 FIRST_POOL_BATCH = 3
 SEG_P_COLS = N // 8
+SEG_S_POOL_COLS = 96
+SEG_V_POOL_HALF = (N // 2 - SEG_S_POOL_COLS) // 2
+LAST = UNITS - 1
 FIRST_LATE_UNIT = UNITS - 4
 
 
@@ -93,9 +96,13 @@ def tile_featuremaptransformer_pb_t_kernel(tc, q_ir, irSegF, Wk_dr, bk_dr, out):
                 regroup("gpsimd", seg_raw[b], grouped(seg_g, b, "seg_g"), piece * SEG_P_COLS, (piece + 1) * SEG_P_COLS)
 
         def regroup_seg(part, b):
-            if FIRST_POOL_BATCH <= b < B and part > 0:
-                c0 = N // 2 + (part - 1) * N // 4
-                regroup("vector", seg_raw[b], grouped(seg_g, b, "seg_g"), c0, c0 + N // 4)
+            if FIRST_POOL_BATCH <= b < B:
+                dst = grouped(seg_g, b, "seg_g")
+                if part == 0:
+                    regroup("scalar", seg_raw[b], dst, N // 2, N // 2 + SEG_S_POOL_COLS)
+                else:
+                    c0 = N // 2 + SEG_S_POOL_COLS + (part - 1) * SEG_V_POOL_HALF
+                    regroup("vector", seg_raw[b], dst, c0, c0 + SEG_V_POOL_HALF)
             if 0 <= b < FIRST_POOL_BATCH:
                 dst = grouped(seg_g, b, "seg_g")
                 if part == 0:
@@ -181,31 +188,40 @@ def tile_featuremaptransformer_pb_t_kernel(tc, q_ir, irSegF, Wk_dr, bk_dr, out):
                 rsum[u] = stat.tile([P, 1], F32, name="rsum")
                 nc.vector.reciprocal(out=rsum[u][:], in_=ssum[u][:])
 
-        def normalise(engine, u):
+        def normalise(engine, u, i0=0, i1=4):
             if 0 <= u < UNITS:
-                en[u] = epool.tile([P, N], F32, name="en")
+                if i0 == 0:
+                    en[u] = epool.tile([P, N], F32, name="en")
+                part = slice(i0 * P, i1 * P)
                 if engine == "vector":
-                    nc.vector.tensor_scalar_mul(out=en[u][:], in0=e[u][:], scalar1=rsum[u][:])
+                    nc.vector.tensor_scalar_mul(out=en[u][:, part], in0=e[u][:, part], scalar1=rsum[u][:])
                 else:
                     nc.gpsimd.tensor_scalar(
-                        out=en[u][:], in0=e[u][:], scalar1=rsum[u][:], scalar2=0.0, op0=ALU.mult, op1=ALU.add
+                        out=en[u][:, part], in0=e[u][:, part], scalar1=rsum[u][:], scalar2=0.0, op0=ALU.mult, op1=ALU.add
                     )
 
-        def transposes(u):
+        def transposes(u, i0=0, i1=4):
             if 0 <= u < UNITS:
-                tp[u] = pst.tile([P, 512], F32, name="tp")
-                for i in range(4):
-                    nc.tensor.transpose(tp[u][:, i * P : (i + 1) * P], en[u][:, i * P : (i + 1) * P], ident[:])
+                if i1 - i0 == 4:
+                    tp[u, i0] = pst.tile([P, 512], F32, name="tp")
+                else:
+                    tp[u, i0] = psk.tile([P, 512], F32, name="kp")
+                for i in range(i0, i1):
+                    nc.tensor.transpose(tp[u, i0][:, (i - i0) * P : (i - i0 + 1) * P], en[u][:, i * P : (i + 1) * P], ident[:])
 
-        def out_copy_and_store(u):
+        def out_copy_and_store(engine, u, i0=0, i1=4):
             if 0 <= u < UNITS:
                 b = u // 4
                 cols = slice((u % 4) * P, (u % 4 + 1) * P)
                 if u % 4 == 0:
                     ot[b] = opool.tile([P, 4, N], F32, name="ot")
-                nc.scalar.copy(out=ot[b][:, :, cols], in_=tp[u][:].rearrange("p (i m) -> p i m", i=4))
+                bank = tp[u, i0][:, : (i1 - i0) * P].rearrange("p (i m) -> p i m", i=i1 - i0)
+                if engine == "vector":
+                    nc.vector.tensor_copy(out=ot[b][:, i0:i1, cols], in_=bank)
+                else:
+                    nc.scalar.copy(out=ot[b][:, i0:i1, cols], in_=bank)
                 rows = out[b].rearrange("(i p) m -> p i m", p=P)
-                nc.sync.dma_start(out=rows[:, :, cols], in_=ot[b][:, :, cols])
+                nc.sync.dma_start(out=rows[:, i0:i1, cols], in_=ot[b][:, i0:i1, cols])
 
         w_words = w_raw[:].bitcast(F32).rearrange("p (t w u) -> p t u w", t=PACK, u=2)
         w_grp = const.tile([P, PACK * C], BF16, name="w_grp", align_bytes=64)
@@ -247,16 +263,29 @@ def tile_featuremaptransformer_pb_t_kernel(tc, q_ir, irSegF, Wk_dr, bk_dr, out):
             row_max(v)
             if late:
                 reciprocal(s - 1)
-                normalise("vector", s - 1)
+                for i0 in range(0, 4, 2 if s - 1 == LAST else 4):
+                    normalise("vector", s - 1, i0, i0 + (2 if s - 1 == LAST else 4))
+            if s - 2 == LAST - 1:
+                out_copy_and_store("vector", s - 2)
             key_out(v + 2)
             if not late:
                 normalise("gpsimd", s - 1)
             regroup_seg_pool((v + 10) % 4, (v + 10) // 4)
             exponent(s)
-            out_copy_and_store(s - 2)
-            if j == 2 and b + 2 > 0:
+            if s - 2 == LAST:
+                out_copy_and_store("scalar", s - 2, 0, 2)
+                out_copy_and_store("scalar", s - 2, 2, 4)
+            elif s - 2 != LAST - 1:
+                out_copy_and_store("scalar", s - 2)
+            if j == 2 and 0 < b + 2 < FIRST_POOL_BATCH:
                 regroup_seg(0, b + 2)
+            if j == 2 and b + 3 >= FIRST_POOL_BATCH:
+                regroup_seg(0, b + 3)
             regroup_q(v + 8)
             key_matmul(v + 3)
             score_matmul(v + 1)
-            transposes(s - 1)
+            if s - 1 == LAST:
+                transposes(s - 1, 0, 2)
+                transposes(s - 1, 2, 4)
+            else:
+                transposes(s - 1)

@@ -87,7 +87,14 @@ def tile_featuremaptransformer_pb_t_kernel(tc, q_ir, irSegF, Wk_dr, bk_dr, out):
             if engine == "scalar":
                 nc.scalar.copy(out=dst, in_=src)
             elif engine == "gpsimd":
-                nc.gpsimd.tensor_scalar(out=dst, in0=src, scalar1=1.0, scalar2=0.0, op0=ALU.mult, op1=ALU.add)
+                nc.gpsimd.tensor_scalar(
+                    out=dst_tile[:, c0 * PACK : c1 * PACK].rearrange("p (n t) -> p n t", t=PACK),
+                    in0=src_tile[:].rearrange("p (t n) -> p n t", t=PACK)[:, c0:c1, :],
+                    scalar1=1.0,
+                    scalar2=0.0,
+                    op0=ALU.mult,
+                    op1=ALU.add,
+                )
             else:
                 nc.vector.tensor_copy(out=dst, in_=src)
 
@@ -260,6 +267,7 @@ def tile_featuremaptransformer_pb_t_kernel(tc, q_ir, irSegF, Wk_dr, bk_dr, out):
             late = s - 1 >= FIRST_LATE_UNIT
             if not late:
                 reciprocal(s - 1)
+            key_out(v + 2)
             row_max(v)
             if late:
                 reciprocal(s - 1)
@@ -267,7 +275,6 @@ def tile_featuremaptransformer_pb_t_kernel(tc, q_ir, irSegF, Wk_dr, bk_dr, out):
                     normalise("vector", s - 1, i0, i0 + (2 if s - 1 == LAST else 4))
             if s - 2 == LAST - 1:
                 out_copy_and_store("vector", s - 2)
-            key_out(v + 2)
             if not late:
                 normalise("gpsimd", s - 1)
             regroup_seg_pool((v + 10) % 4, (v + 10) // 4)

@@ -24,8 +24,10 @@ SEG_S_COLS = 128
 SEG_V_HALF = (N - SEG_S_COLS) // 2
 FIRST_POOL_BATCH = 3
 SEG_P_COLS = N // 8
-SEG_S_POOL_COLS = 96
+SEG_S_POOL_COLS = 32
 SEG_V_POOL_HALF = (N // 2 - SEG_S_POOL_COLS) // 2
+HEAD_Q_V_BLOCKS = (2, 3)
+HEAD_Q_V_STEP = -4
 LAST = UNITS - 1
 FIRST_LATE_UNIT = UNITS - 4
 
@@ -118,9 +120,9 @@ def tile_featuremaptransformer_pb_t_kernel(tc, q_ir, irSegF, Wk_dr, bk_dr, out):
                     c0 = SEG_S_COLS + (part - 1) * SEG_V_HALF
                     regroup("vector", seg_raw[b], dst, c0, c0 + SEG_V_HALF)
 
-        def regroup_q(k):
+        def regroup_q(engine, k):
             if 0 <= k < UNITS:
-                regroup("scalar", q_raw[k // 4], grouped(q_g, k // 4, "q_g"), (k % 4) * P, (k % 4 + 1) * P)
+                regroup(engine, q_raw[k // 4], grouped(q_g, k // 4, "q_g"), (k % 4) * P, (k % 4 + 1) * P)
 
         def quantise(src, dst, b, name):
             if 0 <= b < B:
@@ -245,8 +247,8 @@ def tile_featuremaptransformer_pb_t_kernel(tc, q_ir, irSegF, Wk_dr, bk_dr, out):
             dst = w_grp_f[:, h * 512 : (h + 1) * 512].rearrange("p (t c u) -> p t c u", t=2, u=2)
             src = wt[h][:].rearrange("p (t u c) -> p t c u", t=2, u=2)
             nc.scalar.copy(out=dst, in_=src)
-        for part in range(3):
-            regroup_seg(part, 0)
+        for half in range(2):
+            regroup("vector", seg_raw[0], grouped(seg_g, 0, "seg_g"), half * N // 2, (half + 1) * N // 2)
         w_code = const.tile([P, C], U32, name="w_code", align_bytes=64)
         w_scale = const.tile([P, C], U8, name="w_scale", align_bytes=64)
         nc.vector.quantize_mx(out=w_code[:].bitcast(FP8X4), scales=w_scale[:], in_=w_grp[:])
@@ -257,6 +259,9 @@ def tile_featuremaptransformer_pb_t_kernel(tc, q_ir, irSegF, Wk_dr, bk_dr, out):
             b, j = v // 4, v % 4
             if j == 0:
                 quantise(seg_g, seg_mx, b + 1, "seg")
+            if v == HEAD_Q_V_STEP:
+                for k in HEAD_Q_V_BLOCKS:
+                    regroup_q("vector", k)
             if j == 1 and b + 2 > 0:
                 regroup_seg(1, b + 2)
             if j == 2:
@@ -288,7 +293,8 @@ def tile_featuremaptransformer_pb_t_kernel(tc, q_ir, irSegF, Wk_dr, bk_dr, out):
                 regroup_seg(0, b + 2)
             if j == 2 and b + 3 >= FIRST_POOL_BATCH:
                 regroup_seg(0, b + 3)
-            regroup_q(v + 8)
+            if v + 8 not in HEAD_Q_V_BLOCKS:
+                regroup_q("scalar", v + 8)
             key_matmul(v + 3)
             score_matmul(v + 1)
             if s - 1 == LAST:

@@ -24,8 +24,7 @@ SEG_S_COLS = 128
 SEG_V_HALF = (N - SEG_S_COLS) // 2
 FIRST_POOL_BATCH = 3
 SEG_P_COLS = N // 8
-SEG_S_POOL_COLS = 32
-SEG_V_POOL_HALF = (N // 2 - SEG_S_POOL_COLS) // 2
+SEG_S_POOL_PIECE = 96
 HEAD_Q_V_BLOCKS = (2, 3)
 HEAD_Q_V_STEP = -4
 LAST = UNITS - 1
@@ -45,7 +44,8 @@ def tile_featuremaptransformer_pb_t_kernel(tc, q_ir, irSegF, Wk_dr, bk_dr, out):
         opool = ctx.enter_context(tc.tile_pool(name="opool", bufs=3))
         psk = ctx.enter_context(tc.psum_pool(name="psk", bufs=2))
         pss = ctx.enter_context(tc.psum_pool(name="pss", bufs=3))
-        pst = ctx.enter_context(tc.psum_pool(name="pst", bufs=3))
+        pst = ctx.enter_context(tc.psum_pool(name="pst", bufs=2))
+        psq = ctx.enter_context(tc.psum_pool(name="psq", bufs=1))
         ctx.enter_context(tc.manual_schedule())
 
         bias_bf = const.tile([P, PACK], BF16, name="bias_bf")
@@ -70,12 +70,14 @@ def tile_featuremaptransformer_pb_t_kernel(tc, q_ir, irSegF, Wk_dr, bk_dr, out):
         nc.scalar.activation(out=warm_out[:], in_=warm_in[:], func=ACT.Exp)
         ident = const.tile([P, P], F32, name="ident")
         make_identity(nc, ident[:])
+        ident_bf = const.tile([P, P], BF16, name="ident_bf")
+        make_identity(nc, ident_bf[:])
         bias_f = const.tile([P, PACK], F32, name="bias_f")
         bias_bc = bias_f[:].unsqueeze(1).to_broadcast([P, P, PACK])
 
         seg_g, q_g, key_g = {}, {}, {}
         seg_mx, q_mx, key_mx = {}, {}, {}
-        kp, sp, tp = {}, {}, {}
+        kp, sp, tp, qp = {}, {}, {}, {}
         nmax, ssum, rsum, e, en, ot = {}, {}, {}, {}, {}, {}
 
         def grouped(store, b, name):
@@ -108,10 +110,11 @@ def tile_featuremaptransformer_pb_t_kernel(tc, q_ir, irSegF, Wk_dr, bk_dr, out):
             if FIRST_POOL_BATCH <= b < B:
                 dst = grouped(seg_g, b, "seg_g")
                 if part == 0:
-                    regroup("scalar", seg_raw[b], dst, N // 2, N // 2 + SEG_S_POOL_COLS)
-                else:
-                    c0 = N // 2 + SEG_S_POOL_COLS + (part - 1) * SEG_V_POOL_HALF
-                    regroup("vector", seg_raw[b], dst, c0, c0 + SEG_V_POOL_HALF)
+                    regroup("scalar", seg_raw[b], dst, N // 2, N // 2 + SEG_S_POOL_PIECE)
+                if part == 3:
+                    regroup("scalar", seg_raw[b], dst, N // 2 + SEG_S_POOL_PIECE, N // 2 + 2 * SEG_S_POOL_PIECE)
+                if part == 1:
+                    regroup("vector", seg_raw[b], dst, N // 2 + 2 * SEG_S_POOL_PIECE, N)
             if 0 <= b < FIRST_POOL_BATCH:
                 dst = grouped(seg_g, b, "seg_g")
                 if part == 0:
@@ -123,6 +126,25 @@ def tile_featuremaptransformer_pb_t_kernel(tc, q_ir, irSegF, Wk_dr, bk_dr, out):
         def regroup_q(engine, k):
             if 0 <= k < UNITS:
                 regroup(engine, q_raw[k // 4], grouped(q_g, k // 4, "q_g"), (k % 4) * P, (k % 4 + 1) * P)
+
+        def q_matmul(b, half):
+            if FIRST_POOL_BATCH <= b < B:
+                qp[b, half] = psq.tile([P, 2 * PACK * P], BF16, name="qp")
+                view = q_raw[b][:].rearrange("p (t n) -> p n t", t=PACK)
+                for i in range(2):
+                    blk = 2 * half + i
+                    nc.tensor.matmul(
+                        out=qp[b, half][:, i * PACK * P : (i + 1) * PACK * P],
+                        lhsT=ident_bf[:],
+                        rhs=view[:, blk * P : (blk + 1) * P, :],
+                        start=True,
+                        stop=True,
+                    )
+
+        def q_copy(b, half):
+            if FIRST_POOL_BATCH <= b < B:
+                dst = grouped(q_g, b, "q_g")
+                nc.scalar.copy(out=dst[:, half * 2 * PACK * P : (half + 1) * 2 * PACK * P], in_=qp[b, half][:])
 
         def quantise(src, dst, b, name):
             if 0 <= b < B:
@@ -291,12 +313,20 @@ def tile_featuremaptransformer_pb_t_kernel(tc, q_ir, irSegF, Wk_dr, bk_dr, out):
                 out_copy_and_store("scalar", s - 2)
             if j == 2 and 0 < b + 2 < FIRST_POOL_BATCH:
                 regroup_seg(0, b + 2)
-            if j == 2 and b + 3 >= FIRST_POOL_BATCH:
+            if j == 1 and b + 3 >= FIRST_POOL_BATCH:
                 regroup_seg(0, b + 3)
-            if v + 8 not in HEAD_Q_V_BLOCKS:
+            if j == 3 and b + 3 >= FIRST_POOL_BATCH:
+                regroup_seg(3, b + 3)
+            if b + 2 < FIRST_POOL_BATCH and v + 8 not in HEAD_Q_V_BLOCKS:
                 regroup_q("scalar", v + 8)
+            if j % 2 == 0:
+                q_copy(b + 2, j // 2)
             key_matmul(v + 3)
             score_matmul(v + 1)
+            if j == 3:
+                q_matmul(b + 3, 0)
+            if j == 1:
+                q_matmul(b + 2, 1)
             if s - 1 == LAST:
                 transposes(s - 1, 0, 2)
                 transposes(s - 1, 2, 4)

@@ -23,8 +23,8 @@ FLOPS = 2 * 2 * B * C * N * N
 SEG_S_COLS = 128
 SEG_V_HALF = (N - SEG_S_COLS) // 2
 FIRST_POOL_BATCH = 3
-SEG_P_COLS = N // 8
-SEG_S_POOL_PIECE = 96
+SEG_P_COLS = 56
+SEG_S_POOL_PIECE = (N - 4 * SEG_P_COLS) // 2
 HEAD_Q_V_BLOCKS = (2, 3)
 HEAD_Q_V_STEP = -4
 LAST = UNITS - 1
@@ -110,11 +110,9 @@ def tile_featuremaptransformer_pb_t_kernel(tc, q_ir, irSegF, Wk_dr, bk_dr, out):
             if FIRST_POOL_BATCH <= b < B:
                 dst = grouped(seg_g, b, "seg_g")
                 if part == 0:
-                    regroup("scalar", seg_raw[b], dst, N // 2, N // 2 + SEG_S_POOL_PIECE)
+                    regroup("scalar", seg_raw[b], dst, 4 * SEG_P_COLS, 4 * SEG_P_COLS + SEG_S_POOL_PIECE)
                 if part == 3:
-                    regroup("scalar", seg_raw[b], dst, N // 2 + SEG_S_POOL_PIECE, N // 2 + 2 * SEG_S_POOL_PIECE)
-                if part == 1:
-                    regroup("vector", seg_raw[b], dst, N // 2 + 2 * SEG_S_POOL_PIECE, N)
+                    regroup("scalar", seg_raw[b], dst, 4 * SEG_P_COLS + SEG_S_POOL_PIECE, N)
             if 0 <= b < FIRST_POOL_BATCH:
                 dst = grouped(seg_g, b, "seg_g")
                 if part == 0:

@@ -24,6 +24,8 @@ SEG_S_COLS = 128
 SEG_V_HALF = (N - SEG_S_COLS) // 2
 FIRST_POOL_BATCH = 3
 SEG_P_COLS = 56
+S_PIECES = (112, 112)
+V_PIECES = (64,)
 SEG_S_POOL_PIECE = (N - 4 * SEG_P_COLS) // 2
 HEAD_Q_V_BLOCKS = (2, 3)
 HEAD_Q_V_STEP = -4
@@ -109,10 +111,16 @@ def tile_featuremaptransformer_pb_t_kernel(tc, q_ir, irSegF, Wk_dr, bk_dr, out):
         def regroup_seg(part, b):
             if FIRST_POOL_BATCH <= b < B:
                 dst = grouped(seg_g, b, "seg_g")
-                if part == 0:
-                    regroup("scalar", seg_raw[b], dst, 4 * SEG_P_COLS, 4 * SEG_P_COLS + SEG_S_POOL_PIECE)
-                if part == 3:
-                    regroup("scalar", seg_raw[b], dst, 4 * SEG_P_COLS + SEG_S_POOL_PIECE, N)
+                c0 = 4 * SEG_P_COLS
+                if part == 0 and len(S_PIECES) > 0:
+                    regroup("scalar", seg_raw[b], dst, c0, c0 + S_PIECES[0])
+                if part == 3 and len(S_PIECES) > 1:
+                    regroup("scalar", seg_raw[b], dst, c0 + S_PIECES[0], c0 + sum(S_PIECES))
+                c0 = c0 + sum(S_PIECES)
+                if part == 1 and len(V_PIECES) > 0:
+                    regroup("vector", seg_raw[b], dst, c0, c0 + V_PIECES[0])
+                if part == 2 and len(V_PIECES) > 1:
+                    regroup("vector", seg_raw[b], dst, c0 + V_PIECES[0], c0 + sum(V_PIECES))
             if 0 <= b < FIRST_POOL_BATCH:
                 dst = grouped(seg_g, b, "seg_g")
                 if part == 0:

@@ -28,7 +28,7 @@ S_PIECES = (112, 112)
 V_PIECES = (64,)
 SEG_S_POOL_PIECE = (N - 4 * SEG_P_COLS) // 2
 HEAD_Q_V_BLOCKS = (2, 3)
-HEAD_Q_V_STEP = -4
+HEAD_SEG_S_COLS = 128
 LAST = UNITS - 1
 FIRST_LATE_UNIT = UNITS - 4
 
@@ -54,14 +54,15 @@ def tile_featuremaptransformer_pb_t_kernel(tc, q_ir, irSegF, Wk_dr, bk_dr, out):
         nc.scalar.dma_start(out=bias_bf[:], in_=bk_dr.rearrange("(p t) -> p t", t=PACK))
         w_raw = const.tile([P, PACK * C], BF16, name="w_raw")
         w_rows = Wk_dr.rearrange("(p t) c -> p (t c)", t=PACK)
-        for h in range(2):
-            nc.sync.dma_start(out=w_raw[:, h * 2 * C : (h + 1) * 2 * C], in_=w_rows[:, h * 2 * C : (h + 1) * 2 * C])
+        nc.sync.dma_start(out=w_raw[:, : 2 * C], in_=w_rows[:, : 2 * C])
         seg_raw = []
         q_raw = []
         for b in range(B):
             sr = raw.tile([P, PACK * N], BF16, name="seg_raw%d" % b)
             nc.sync.dma_start(out=sr[:], in_=irSegF[b].rearrange("(p t) h w -> p (t h w)", t=PACK))
             seg_raw.append(sr)
+            if b == 0:
+                nc.sync.dma_start(out=w_raw[:, 2 * C :], in_=w_rows[:, 2 * C :])
             qr = raw.tile([P, PACK * N], BF16, name="q_raw%d" % b)
             nc.sync.dma_start(out=qr[:], in_=q_ir[b].rearrange("(p t) n -> p (t n)", t=PACK))
             q_raw.append(qr)
@@ -123,11 +124,15 @@ def tile_featuremaptransformer_pb_t_kernel(tc, q_ir, irSegF, Wk_dr, bk_dr, out):
                     regroup("vector", seg_raw[b], dst, c0 + V_PIECES[0], c0 + sum(V_PIECES))
             if 0 <= b < FIRST_POOL_BATCH:
                 dst = grouped(seg_g, b, "seg_g")
-                if part == 0:
+                s_cols = 2 * SEG_S_COLS if b == 1 else SEG_S_COLS
+                v_half = (N - s_cols) // 2
+                if part == 4:
+                    regroup("scalar", seg_raw[b], dst, SEG_S_COLS, 2 * SEG_S_COLS)
+                elif part == 0:
                     regroup("scalar", seg_raw[b], dst, 0, SEG_S_COLS)
                 else:
-                    c0 = SEG_S_COLS + (part - 1) * SEG_V_HALF
-                    regroup("vector", seg_raw[b], dst, c0, c0 + SEG_V_HALF)
+                    c0 = s_cols + (part - 1) * v_half
+                    regroup("vector", seg_raw[b], dst, c0, c0 + v_half)
 
         def regroup_q(engine, k):
             if 0 <= k < UNITS:
@@ -275,21 +280,24 @@ def tile_featuremaptransformer_pb_t_kernel(tc, q_ir, irSegF, Wk_dr, bk_dr, out):
             dst = w_grp_f[:, h * 512 : (h + 1) * 512].rearrange("p (t c u) -> p t c u", t=2, u=2)
             src = wt[h][:].rearrange("p (t u c) -> p t c u", t=2, u=2)
             nc.scalar.copy(out=dst, in_=src)
+            if h == 0:
+                regroup("scalar", seg_raw[0], grouped(seg_g, 0, "seg_g"), N - HEAD_SEG_S_COLS, N)
         for half in range(2):
-            regroup("vector", seg_raw[0], grouped(seg_g, 0, "seg_g"), half * N // 2, (half + 1) * N // 2)
+            regroup("vector", seg_raw[0], grouped(seg_g, 0, "seg_g"), half * (N - HEAD_SEG_S_COLS) // 2, (half + 1) * (N - HEAD_SEG_S_COLS) // 2)
         w_code = const.tile([P, C], U32, name="w_code", align_bytes=64)
         w_scale = const.tile([P, C], U8, name="w_scale", align_bytes=64)
-        nc.vector.quantize_mx(out=w_code[:].bitcast(FP8X4), scales=w_scale[:], in_=w_grp[:])
         nc.vector.tensor_copy(out=bias_f[:], in_=bias_bf[:])
+        nc.vector.quantize_mx(out=w_code[:, : C // 2].bitcast(FP8X4), scales=w_scale[:, : C // 2], in_=w_grp[:, : 2 * C])
+        quantise(seg_g, seg_mx, 0, "seg")
+        for k in HEAD_Q_V_BLOCKS:
+            regroup_q("vector", k)
+        nc.vector.quantize_mx(out=w_code[:, C // 2 :].bitcast(FP8X4), scales=w_scale[:, C // 2 :], in_=w_grp[:, 2 * C :])
 
         for s in range(-9, UNITS + 3):
             v = s + 1
             b, j = v // 4, v % 4
-            if j == 0:
+            if j == 0 and b + 1 > 0:
                 quantise(seg_g, seg_mx, b + 1, "seg")
-            if v == HEAD_Q_V_STEP:
-                for k in HEAD_Q_V_BLOCKS:
-                    regroup_q("vector", k)
             if j == 1 and b + 2 > 0:
                 regroup_seg(1, b + 2)
             if j == 2:
@@ -325,6 +333,8 @@ def tile_featuremaptransformer_pb_t_kernel(tc, q_ir, irSegF, Wk_dr, bk_dr, out):
                 regroup_seg(3, b + 3)
             if b + 2 < FIRST_POOL_BATCH and v + 8 not in HEAD_Q_V_BLOCKS:
                 regroup_q("scalar", v + 8)
+            if v + 8 == 1:
+                regroup_seg(4, 1)
             if j % 2 == 0:
                 q_copy(b + 2, j // 2)
             key_matmul(v + 3)

@@ -22,6 +22,7 @@ FLOPS = 2 * 2 * B * C * N * N
 
 SEG_S_COLS = 128
 SEG_V_HALF = (N - SEG_S_COLS) // 2
+FIRST_PE_BATCH = 2
 FIRST_POOL_BATCH = 3
 SEG_P_COLS = 56
 S_PIECES = (112, 112)
@@ -124,10 +125,10 @@ def tile_featuremaptransformer_pb_t_kernel(tc, q_ir, irSegF, Wk_dr, bk_dr, out):
                     regroup("vector", seg_raw[b], dst, c0 + V_PIECES[0], c0 + sum(V_PIECES))
             if 0 <= b < FIRST_POOL_BATCH:
                 dst = grouped(seg_g, b, "seg_g")
-                s_cols = 2 * SEG_S_COLS if b == 1 else SEG_S_COLS
+                s_cols = (b + 1) * SEG_S_COLS
                 v_half = (N - s_cols) // 2
-                if part == 4:
-                    regroup("scalar", seg_raw[b], dst, SEG_S_COLS, 2 * SEG_S_COLS)
+                if part >= 4:
+                    regroup("scalar", seg_raw[b], dst, (part - 3) * SEG_S_COLS, (part - 2) * SEG_S_COLS)
                 elif part == 0:
                     regroup("scalar", seg_raw[b], dst, 0, SEG_S_COLS)
                 else:
@@ -139,7 +140,7 @@ def tile_featuremaptransformer_pb_t_kernel(tc, q_ir, irSegF, Wk_dr, bk_dr, out):
                 regroup(engine, q_raw[k // 4], grouped(q_g, k // 4, "q_g"), (k % 4) * P, (k % 4 + 1) * P)
 
         def q_matmul(b, half):
-            if FIRST_POOL_BATCH <= b < B:
+            if FIRST_PE_BATCH <= b < B:
                 qp[b, half] = psq.tile([P, 2 * PACK * P], BF16, name="qp")
                 view = q_raw[b][:].rearrange("p (t n) -> p n t", t=PACK)
                 for i in range(2):
@@ -153,7 +154,7 @@ def tile_featuremaptransformer_pb_t_kernel(tc, q_ir, irSegF, Wk_dr, bk_dr, out):
                     )
 
         def q_copy(b, half):
-            if FIRST_POOL_BATCH <= b < B:
+            if FIRST_PE_BATCH <= b < B:
                 dst = grouped(q_g, b, "q_g")
                 nc.scalar.copy(out=dst[:, half * 2 * PACK * P : (half + 1) * 2 * PACK * P], in_=qp[b, half][:])
 
@@ -331,10 +332,12 @@ def tile_featuremaptransformer_pb_t_kernel(tc, q_ir, irSegF, Wk_dr, bk_dr, out):
                 regroup_seg(0, b + 3)
             if j == 3 and b + 3 >= FIRST_POOL_BATCH:
                 regroup_seg(3, b + 3)
-            if b + 2 < FIRST_POOL_BATCH and v + 8 not in HEAD_Q_V_BLOCKS:
+            if b + 2 < FIRST_PE_BATCH and v + 8 not in HEAD_Q_V_BLOCKS:
                 regroup_q("scalar", v + 8)
             if v + 8 == 1:
                 regroup_seg(4, 1)
+            if v == 0 or v == 1:
+                regroup_seg(4 + v, 2)
             if j % 2 == 0:
                 q_copy(b + 2, j // 2)
             key_matmul(v + 3)

from contextlib import ExitStack

import concourse.mybir as mybir
from concourse.masks import make_identity

F32 = mybir.dt.float32
BF16 = mybir.dt.bfloat16
U32 = mybir.dt.uint32
U8 = mybir.dt.uint8
FP8X4 = mybir.dt.float8_e4m3fn_x4
ALU = mybir.AluOpType
ACT = mybir.ActivationFunctionType
AX = mybir.AxisListType

P = 128
B = 8
C = 512
N = 512
PACK = 4
UNITS = 4 * B
FLOPS = 2 * 2 * B * C * N * N

SEG_S_COLS = 128
SEG_V_HALF = (N - SEG_S_COLS) // 2
FIRST_PE_BATCH = 2
FIRST_POOL_BATCH = 3
SEG_P_COLS = 56
S_PIECES = (112, 112)
V_PIECES = (64,)
SEG_S_POOL_PIECE = (N - 4 * SEG_P_COLS) // 2
HEAD_Q_V_BLOCKS = (2, 3)
HEAD_SEG_S_COLS = 128
LAST = UNITS - 1
FIRST_LATE_UNIT = UNITS - 4


def tile_featuremaptransformer_pb_t_kernel(tc, q_ir, irSegF, Wk_dr, bk_dr, out):
    nc = tc.nc
    with ExitStack() as ctx:
        const = ctx.enter_context(tc.tile_pool(name="const", bufs=1))
        raw = ctx.enter_context(tc.tile_pool(name="raw", bufs=1))
        grp = ctx.enter_context(tc.tile_pool(name="grp", bufs=3))
        wrd = ctx.enter_context(tc.tile_pool(name="wrd", bufs=3))
        keyp = ctx.enter_context(tc.tile_pool(name="keyp", bufs=4))
        stat = ctx.enter_context(tc.tile_pool(name="stat", bufs=8))
        epool = ctx.enter_context(tc.tile_pool(name="epool", bufs=4))
        opool = ctx.enter_context(tc.tile_pool(name="opool", bufs=3))
        psk = ctx.enter_context(tc.psum_pool(name="psk", bufs=2))
        pss = ctx.enter_context(tc.psum_pool(name="pss", bufs=3))
        pst = ctx.enter_context(tc.psum_pool(name="pst", bufs=2))
        psq = ctx.enter_context(tc.psum_pool(name="psq", bufs=1))
        ctx.enter_context(tc.manual_schedule())

        bias_bf = const.tile([P, PACK], BF16, name="bias_bf")
        nc.scalar.dma_start(out=bias_bf[:], in_=bk_dr.rearrange("(p t) -> p t", t=PACK))
        w_raw = const.tile([P, PACK * C], BF16, name="w_raw")
        w_rows = Wk_dr.rearrange("(p t) c -> p (t c)", t=PACK)
        nc.sync.dma_start(out=w_raw[:, : 2 * C], in_=w_rows[:, : 2 * C])
        seg_raw = []
        q_raw = []
        for b in range(B):
            sr = raw.tile([P, PACK * N], BF16, name="seg_raw%d" % b)
            nc.sync.dma_start(out=sr[:], in_=irSegF[b].rearrange("(p t) h w -> p (t h w)", t=PACK))
            seg_raw.append(sr)
            if b == 0:
                nc.sync.dma_start(out=w_raw[:, 2 * C :], in_=w_rows[:, 2 * C :])
            qr = raw.tile([P, PACK * N], BF16, name="q_raw%d" % b)
            nc.sync.dma_start(out=qr[:], in_=q_ir[b].rearrange("(p t) n -> p (t n)", t=PACK))
            q_raw.append(qr)

        warm_in = const.tile([P, 1], F32, name="warm_in")
        warm_out = const.tile([P, 1], F32, name="warm_out")
        nc.vector.memset(warm_in[:], 0.0)
        nc.scalar.activation(out=warm_out[:], in_=warm_in[:], func=ACT.Exp)
        ident = const.tile([P, P], F32, name="ident")
        make_identity(nc, ident[:])
        ident_bf = const.tile([P, P], BF16, name="ident_bf")
        make_identity(nc, ident_bf[:])
        bias_f = const.tile([P, PACK], F32, name="bias_f")
        bias_bc = bias_f[:].unsqueeze(1).to_broadcast([P, P, PACK])

        seg_g, q_g, key_g = {}, {}, {}
        seg_mx, q_mx, key_mx = {}, {}, {}
        kp, sp, tp, qp = {}, {}, {}, {}
        nmax, ssum, rsum, e, en, ot = {}, {}, {}, {}, {}, {}

        def grouped(store, b, name):
            if b not in store:
                store[b] = grp.tile([P, PACK * N], BF16, name=name, align_bytes=64)
            return store[b]

        def regroup(engine, src_tile, dst_tile, c0, c1):
            dst = dst_tile[:, c0 * PACK : c1 * PACK].rearrange("p (c i t) -> p c t i", i=4, t=PACK)
            src = src_tile[:].rearrange("p (t n) -> p t n", t=PACK)[:, :, c0:c1].rearrange("p t (c i) -> p c t i", i=4)
            if engine == "scalar":
                nc.scalar.copy(out=dst, in_=src)
            elif engine == "gpsimd":
                nc.gpsimd.tensor_scalar(
                    out=dst_tile[:, c0 * PACK : c1 * PACK].rearrange("p (n t) -> p n t", t=PACK),
                    in0=src_tile[:].rearrange("p (t n) -> p n t", t=PACK)[:, c0:c1, :],
                    scalar1=1.0,
                    scalar2=0.0,
                    op0=ALU.mult,
                    op1=ALU.add,
                )
            else:
                nc.vector.tensor_copy(out=dst, in_=src)

        def regroup_seg_pool(piece, b):
            if FIRST_POOL_BATCH <= b < B:
                regroup("gpsimd", seg_raw[b], grouped(seg_g, b, "seg_g"), piece * SEG_P_COLS, (piece + 1) * SEG_P_COLS)

        def regroup_seg(part, b):
            if FIRST_POOL_BATCH <= b < B:
                dst = grouped(seg_g, b, "seg_g")
                c0 = 4 * SEG_P_COLS
                if part == 0 and len(S_PIECES) > 0:
                    regroup("scalar", seg_raw[b], dst, c0, c0 + S_PIECES[0])
                if part == 3 and len(S_PIECES) > 1:
                    regroup("scalar", seg_raw[b], dst, c0 + S_PIECES[0], c0 + sum(S_PIECES))
                c0 = c0 + sum(S_PIECES)
                if part == 1 and len(V_PIECES) > 0:
                    regroup("vector", seg_raw[b], dst, c0, c0 + V_PIECES[0])
                if part == 2 and len(V_PIECES) > 1:
                    regroup("vector", seg_raw[b], dst, c0 + V_PIECES[0], c0 + sum(V_PIECES))
            if 0 <= b < FIRST_POOL_BATCH:
                dst = grouped(seg_g, b, "seg_g")
                s_cols = (b + 1) * SEG_S_COLS
                v_half = (N - s_cols) // 2
                if part >= 4:
                    regroup("scalar", seg_raw[b], dst, (part - 3) * SEG_S_COLS, (part - 2) * SEG_S_COLS)
                elif part == 0:
                    regroup("scalar", seg_raw[b], dst, 0, SEG_S_COLS)
                else:
                    c0 = s_cols + (part - 1) * v_half
                    regroup("vector", seg_raw[b], dst, c0, c0 + v_half)

        def regroup_q(engine, k):
            if 0 <= k < UNITS:
                regroup(engine, q_raw[k // 4], grouped(q_g, k // 4, "q_g"), (k % 4) * P, (k % 4 + 1) * P)

        def q_matmul(b, half):
            if FIRST_PE_BATCH <= b < B:
                qp[b, half] = psq.tile([P, 2 * PACK * P], BF16, name="qp")
                view = q_raw[b][:].rearrange("p (t n) -> p n t", t=PACK)
                for i in range(2):
                    blk = 2 * half + i
                    nc.tensor.matmul(
                        out=qp[b, half][:, i * PACK * P : (i + 1) * PACK * P],
                        lhsT=ident_bf[:],
                        rhs=view[:, blk * P : (blk + 1) * P, :],
                        start=True,
                        stop=True,
                    )

        def q_copy(b, half):
            if FIRST_PE_BATCH <= b < B:
                dst = grouped(q_g, b, "q_g")
                nc.scalar.copy(out=dst[:, half * 2 * PACK * P : (half + 1) * 2 * PACK * P], in_=qp[b, half][:])

        def quantise(src, dst, b, name):
            if 0 <= b < B:
                code = wrd.tile([P, N], U32, name=name + "_code", align_bytes=64)
                scale = wrd.tile([P, N], U8, name=name + "_scale", align_bytes=64)
                nc.vector.quantize_mx(out=code[:].bitcast(FP8X4), scales=scale[:], in_=src[b][:])
                dst[b] = (code, scale)

        def key_matmul(u):
            if 0 <= u < UNITS:
                code, scale = seg_mx[u // 4]
                cols = slice((u % 4) * P, (u % 4 + 1) * P)
                kp[u] = psk.tile([P, 512], F32, name="kp")
                for t in range(PACK):
                    nc.tensor.matmul_mx(
                        out=kp[u][:, t * P : (t + 1) * P],
                        lhsT=w_code[:, t * P : (t + 1) * P].bitcast(FP8X4),
                        lhsT_scale=w_scale[:, t * P : (t + 1) * P],
                        rhs=code[:, cols].bitcast(FP8X4),
                        rhs_scale=scale[:, cols],
                        start=True,
                        stop=True,
                    )

        def key_out(u):
            if 0 <= u < UNITS:
                key_g[u] = keyp.tile([P, PACK * P], BF16, name="key_g", align_bytes=64)
                nc.vector.tensor_tensor(
                    out=key_g[u][:].rearrange("p (m t) -> p m t", t=PACK),
                    in0=kp[u][:].rearrange("p (t m) -> p m t", t=PACK),
                    in1=bias_bc,
                    op=ALU.add,
                )

        def quantise_key(u):
            if 0 <= u < UNITS:
                code = keyp.tile([P, P], U32, name="key_code", align_bytes=64)
                scale = keyp.tile([P, P], U8, name="key_scale", align_bytes=64)
                nc.vector.quantize_mx(out=code[:].bitcast(FP8X4), scales=scale[:], in_=key_g[u][:])
                key_mx[u] = (code, scale)

        def score_matmul(u):
            if 0 <= u < UNITS:
                k_code, k_scale = key_mx[u]
                q_code, q_scale = q_mx[u // 4]
                sp[u] = pss.tile([P, 512], F32, name="sp")
                nc.tensor.matmul_mx(
                    out=sp[u][:],
                    lhsT=k_code[:].bitcast(FP8X4),
                    lhsT_scale=k_scale[:],
                    rhs=q_code[:].bitcast(FP8X4),
                    rhs_scale=q_scale[:],
                    start=True,
                    stop=True,
                )

        def row_max(u):
            if 0 <= u < UNITS:
                nmax[u] = stat.tile([P, 1], F32, name="nmax")
                nc.vector.tensor_reduce(out=nmax[u][:], in_=sp[u][:], axis=AX.X, op=ALU.max, negate=True)

        def exponent(u):
            if 0 <= u < UNITS:
                e[u] = epool.tile([P, N], F32, name="e")
                ssum[u] = stat.tile([P, 1], F32, name="ssum")
                nc.scalar.activation(
                    out=e[u][:], in_=sp[u][:], func=ACT.Exp, bias=nmax[u][:], scale=1.0, accum_out=ssum[u][:]
                )

        def reciprocal(u):
            if 0 <= u < UNITS:
                rsum[u] = stat.tile([P, 1], F32, name="rsum")
                nc.vector.reciprocal(out=rsum[u][:], in_=ssum[u][:])

        def normalise(engine, u, i0=0, i1=4):
            if 0 <= u < UNITS:
                if i0 == 0:
                    en[u] = epool.tile([P, N], F32, name="en")
                part = slice(i0 * P, i1 * P)
                if engine == "vector":
                    nc.vector.tensor_scalar_mul(out=en[u][:, part], in0=e[u][:, part], scalar1=rsum[u][:])
                else:
                    nc.gpsimd.tensor_scalar(
                        out=en[u][:, part], in0=e[u][:, part], scalar1=rsum[u][:], scalar2=0.0, op0=ALU.mult, op1=ALU.add
                    )

        def transposes(u, i0=0, i1=4):
            if 0 <= u < UNITS:
                if i1 - i0 == 4:
                    tp[u, i0] = pst.tile([P, 512], F32, name="tp")
                else:
                    tp[u, i0] = psk.tile([P, 512], F32, name="kp")
                for i in range(i0, i1):
                    nc.tensor.transpose(tp[u, i0][:, (i - i0) * P : (i - i0 + 1) * P], en[u][:, i * P : (i + 1) * P], ident[:])

        def out_copy_and_store(engine, u, i0=0, i1=4):
            if 0 <= u < UNITS:
                b = u // 4
                cols = slice((u % 4) * P, (u % 4 + 1) * P)
                if u % 4 == 0:
                    ot[b] = opool.tile([P, 4, N], F32, name="ot")
                bank = tp[u, i0][:, : (i1 - i0) * P].rearrange("p (i m) -> p i m", i=i1 - i0)
                if engine == "vector":
                    nc.vector.tensor_copy(out=ot[b][:, i0:i1, cols], in_=bank)
                else:
                    nc.scalar.copy(out=ot[b][:, i0:i1, cols], in_=bank)
                rows = out[b].rearrange("(i p) m -> p i m", p=P)
                nc.sync.dma_start(out=rows[:, i0:i1, cols], in_=ot[b][:, i0:i1, cols])

        w_words = w_raw[:].bitcast(F32).rearrange("p (t w u) -> p t u w", t=PACK, u=2)
        w_grp = const.tile([P, PACK * C], BF16, name="w_grp", align_bytes=64)
        w_grp_f = w_grp[:].bitcast(F32)
        wt = []
        for h in range(2):
            wt.append(pst.tile([P, 512], F32, name="wt", tag="tp"))
            for t2 in range(2):
                for u2 in range(2):
                    nc.tensor.transpose(
                        wt[h][:, (t2 * 2 + u2) * P : (t2 * 2 + u2 + 1) * P], w_words[:, 2 * h + t2, u2, :], ident[:]
                    )
        for h in range(2):
            dst = w_grp_f[:, h * 512 : (h + 1) * 512].rearrange("p (t c u) -> p t c u", t=2, u=2)
            src = wt[h][:].rearrange("p (t u c) -> p t c u", t=2, u=2)
            nc.scalar.copy(out=dst, in_=src)
            if h == 0:
                regroup("scalar", seg_raw[0], grouped(seg_g, 0, "seg_g"), N - HEAD_SEG_S_COLS, N)
        for half in range(2):
            regroup("vector", seg_raw[0], grouped(seg_g, 0, "seg_g"), half * (N - HEAD_SEG_S_COLS) // 2, (half + 1) * (N - HEAD_SEG_S_COLS) // 2)
        w_code = const.tile([P, C], U32, name="w_code", align_bytes=64)
        w_scale = const.tile([P, C], U8, name="w_scale", align_bytes=64)
        nc.vector.tensor_copy(out=bias_f[:], in_=bias_bf[:])
        nc.vector.quantize_mx(out=w_code[:, : C // 2].bitcast(FP8X4), scales=w_scale[:, : C // 2], in_=w_grp[:, : 2 * C])
        quantise(seg_g, seg_mx, 0, "seg")
        for k in HEAD_Q_V_BLOCKS:
            regroup_q("vector", k)
        nc.vector.quantize_mx(out=w_code[:, C // 2 :].bitcast(FP8X4), scales=w_scale[:, C // 2 :], in_=w_grp[:, 2 * C :])

        for s in range(-9, UNITS + 3):
            v = s + 1
            b, j = v // 4, v % 4
            if j == 0 and b + 1 > 0:
                quantise(seg_g, seg_mx, b + 1, "seg")
            if j == 1 and b + 2 > 0:
                regroup_seg(1, b + 2)
            if j == 2:
                quantise(q_g, q_mx, b + 1, "q")
            if j == 3 and b + 2 > 0:
                regroup_seg(2, b + 2)
            quantise_key(v + 1)
            late = s - 1 >= FIRST_LATE_UNIT
            if not late:
                reciprocal(s - 1)
            key_out(v + 2)
            row_max(v)
            if late:
                reciprocal(s - 1)
                for i0 in range(0, 4, 2 if s - 1 == LAST else 4):
                    normalise("vector", s - 1, i0, i0 + (2 if s - 1 == LAST else 4))
            if s - 2 == LAST - 1:
                out_copy_and_store("vector", s - 2)
            if not late:
                normalise("gpsimd", s - 1)
            regroup_seg_pool((v + 10) % 4, (v + 10) // 4)
            exponent(s)
            if s - 2 == LAST:
                out_copy_and_store("scalar", s - 2, 0, 2)
                out_copy_and_store("scalar", s - 2, 2, 4)
            elif s - 2 != LAST - 1:
                out_copy_and_store("scalar", s - 2)
            if j == 2 and 0 < b + 2 < FIRST_POOL_BATCH:
                regroup_seg(0, b + 2)
            if j == 1 and b + 3 >= FIRST_POOL_BATCH:
                regroup_seg(0, b + 3)
            if j == 3 and b + 3 >= FIRST_POOL_BATCH:
                regroup_seg(3, b + 3)
            if b + 2 < FIRST_PE_BATCH and v + 8 not in HEAD_Q_V_BLOCKS:
                regroup_q("scalar", v + 8)
            if v + 8 == 1:
                regroup_seg(4, 1)
            if v == 0 or v == 1:
                regroup_seg(4 + v, 2)
            if j % 2 == 0:
                q_copy(b + 2, j // 2)
            key_matmul(v + 3)
            score_matmul(v + 1)
            if j == 3:
                q_matmul(b + 3, 0)
            if j == 1:
                q_matmul(b + 2, 1)
            if s - 1 == LAST:
                transposes(s - 1, 0, 2)
                transposes(s - 1, 2, 4)
            else:
                transposes(s - 1)
